import numpy as np
import ml_dtypes


def mxq(x, axis, fmt="e4m3"):
    dtype, down = {"e4m3": (ml_dtypes.float8_e4m3fn, 7), "e5m2": (ml_dtypes.float8_e5m2, 14)}[fmt]
    v = np.moveaxis(np.asarray(x, np.float32).astype(ml_dtypes.bfloat16).astype(np.float64), axis, -1)
    blocks = v.reshape(v.shape[:-1] + (-1, 32))
    amax = np.abs(blocks).max(-1, keepdims=True)
    byte = np.maximum(np.where(amax > 0, np.frexp(amax)[1] - 1 + 127, 0) - down, 1)
    scale = np.exp2(byte - 127.0)
    codes = (blocks / scale).astype(np.float32).astype(dtype).astype(np.float64)
    return np.moveaxis((codes * scale).reshape(v.shape), -1, axis)


WIDE = False


def mx_kscale(k):
    if not WIDE:
        return np.ones(k)
    levels = np.array([10, -10, 5, -5, 0])
    a = np.random.permutation(np.resize(levels, k // 512 * 4)).reshape(k // 512, 4)
    idx = np.arange(k)
    return np.exp2(a[idx // 512, idx % 128 // 32])


BF16 = ml_dtypes.bfloat16


def bf(x):
    return np.asarray(x, np.float32).astype(BF16)


def f64(x):
    return np.asarray(x).astype(np.float64)


B, S, HIDDEN, HEADS, BLK = 1, 2048, 1024, 8, 512
HEAD = HIDDEN // HEADS


def gammas():
    return 1.0 - np.exp(np.log(2.0) * np.linspace(-9.0, -5.0, HEADS))


def decay(lo, hi):
    diff = np.arange(lo, hi)[:, None] - np.arange(hi)[None, :]
    causal = diff >= 0
    safe = np.where(causal, diff, 0)
    return np.where(causal[None], gammas()[:, None, None] ** safe[None], 0.0)


def setup_inputs():
    s = mx_kscale(S)[None, :, None, None]
    return {"q": bf(np.random.standard_normal((B, S, HEADS, HEAD)) * HEAD ** -0.25),
            "k": bf(np.random.standard_normal((B, S, HEADS, HEAD)) * HEAD ** -0.25 * s),
            "v": bf(np.random.standard_normal((B, S, HEADS, HEAD)) * 0.3 / s)}


def reference(q, k, v):
    qh = f64(q).transpose(0, 2, 1, 3)
    kh = f64(k).transpose(0, 2, 1, 3)
    vq = mxq(f64(v).transpose(0, 2, 1, 3), 2, "e4m3")
    outs = []
    for i in range(S // BLK):
        lo, hi = i * BLK, (i + 1) * BLK
        sc = (qh[:, :, lo:hi] @ kh[:, :, :hi].transpose(0, 1, 3, 2)) * decay(lo, hi)[None]
        outs.append(mxq(sc, 3, "e4m3") @ vq[:, :, :hi])
    return np.concatenate(outs, axis=2).transpose(0, 2, 1, 3)

@@ -1,0 +1,207 @@
+import math
+from contextlib import ExitStack
+
+import concourse.mybir as mybir
+from concourse.masks import make_identity
+
+BF16 = mybir.dt.bfloat16
+F32 = mybir.dt.float32
+I32 = mybir.dt.int32
+U32 = mybir.dt.uint32
+U8 = mybir.dt.uint8
+FP8X4 = mybir.dt.float8_e4m3fn_x4
+ALU = mybir.AluOpType
+ACT = mybir.ActivationFunctionType
+
+SEQ = 2048
+HEADS = 8
+HEAD = 128
+P = 128
+PACK = 4
+SPAN = P * PACK
+N_SPANS = SEQ // SPAN
+PLANES = 2 * PACK
+CELLS = 4
+THIRD = 3
+LAG = 2
+FAR = 1.0e6
+
+FLOPS = 2 * 2 * HEAD * HEADS * SPAN * SPAN * (1 + 2 + 3 + 4)
+
+
+def tile_multiscaleretention_pa_kernel(tc, q, k, v, out):
+    nc = tc.nc
+    q_rows = q.rearrange("b s h d -> (b s) (h d)")
+    k_rows = k.rearrange("b s h d -> (b s) (h d)")
+    v_rows = v.rearrange("b s h d -> (b s) (h d)")
+    out_rows = out.rearrange("b s h d -> (b s) (h d)")
+    gammas = [1.0 - 2.0 ** (-9.0 + 4.0 * h / 7.0) for h in range(HEADS)]
+
+    jobs = [(i, h) for i in range(N_SPANS) for h in range(HEADS)]
+    rounds = []
+    for i, h in jobs:
+        cells = [(r, j) for r in range(PACK) for j in range(i + 1)]
+        for first in range(0, len(cells), CELLS):
+            rounds.append((i, h, cells[first : first + CELLS]))
+
+    with ExitStack() as stack:
+        keep = stack.enter_context(tc.tile_pool(name="keep", bufs=1))
+        raw = stack.enter_context(tc.tile_pool(name="raw", bufs=2))
+        work = stack.enter_context(tc.tile_pool(name="work", bufs=3))
+        psum_flip = stack.enter_context(tc.psum_pool(name="psum_flip", bufs=2))
+        psum_cell = stack.enter_context(tc.psum_pool(name="psum_cell", bufs=CELLS))
+        psum_out = stack.enter_context(tc.psum_pool(name="psum_out", bufs=2))
+        stack.enter_context(tc.manual_schedule())
+
+        identity = keep.tile([P, P], BF16)
+        make_identity(nc, identity[:])
+
+        steps_int = keep.tile([P, P, PLANES], I32)
+        nc.gpsimd.iota(out=steps_int[:], pattern=[[1, P], [-P, PLANES]], base=PACK * P, channel_multiplier=-1)
+        steps = keep.tile([P, P, PLANES], F32)
+        nc.vector.tensor_copy(out=steps[:], in_=steps_int[:])
+        push = keep.tile([P, P, PLANES], F32)
+        nc.vector.tensor_scalar(out=push[:], in0=steps[:], scalar1=0.0, scalar2=FAR, op0=ALU.is_lt, op1=ALU.mult)
+        nc.vector.tensor_tensor(out=steps[:], in0=steps[:], in1=push[:], op=ALU.add)
+
+        q_raw, k_raw, v_raw = {}, {}, {}
+        keys_t, v_codes, v_scales = {}, {}, {}
+        decay = {}
+        queries_t, v_grouped, products = {}, {}, {}
+        banks, grouped, codes, scales = {}, {}, {}, {}
+
+        def load_span(i):
+            rows = slice(i * SPAN, (i + 1) * SPAN)
+            k_in = raw.tile([P, PACK, HEADS * HEAD], BF16)
+            nc.sync.dma_start(out=k_in[:], in_=k_rows[rows, :].rearrange("(t p) c -> p t c", p=P))
+            q_in = raw.tile([P, PACK, HEADS * HEAD], BF16)
+            nc.sync.dma_start(out=q_in[:], in_=q_rows[rows, :].rearrange("(t p) c -> p t c", p=P))
+            v_in = raw.tile([P, PACK, HEADS * HEAD], BF16)
+            nc.sync.dma_start(out=v_in[:], in_=v_rows[rows, :].rearrange("(t p) c -> p t c", p=P))
+            k_raw[i], q_raw[i], v_raw[i] = k_in, q_in, v_in
+            keys_t[i] = keep.tile([P, HEADS, PACK, P], BF16, name="keys_t%d" % i)
+            v_codes[i] = keep.tile([P, HEADS, HEAD], U32, name="v_codes%d" % i, align_bytes=64)
+            v_scales[i] = keep.tile([P, HEADS, HEAD], U8, name="v_scales%d" % i, align_bytes=64)
+
+        def prepare(i, h):
+            cols = slice(h * HEAD, (h + 1) * HEAD)
+            if i == 0:
+                decay[h] = keep.tile([P, P, PLANES], F32, name="decay%d" % h)
+                nc.scalar.activation(out=decay[h][:], in_=steps[:], func=ACT.Exp, scale=math.log(gammas[h]))
+            flipped = psum_flip.tile([P, 2 * PACK, P], BF16)
+            for t in range(PACK):
+                nc.tensor.transpose(flipped[:, t, :], k_raw[i][:, t, cols], identity[:])
+            for t in range(PACK):
+                nc.tensor.transpose(flipped[:, PACK + t, :], q_raw[i][:, t, cols], identity[:])
+            nc.scalar.copy(out=keys_t[i][:, h], in_=flipped[:, 0:PACK, :])
+            q_t = work.tile([P, PACK, P], BF16)
+            nc.scalar.copy(out=q_t[:], in_=flipped[:, PACK : 2 * PACK, :])
+            queries_t[(i, h)] = q_t
+
+        def regroup_values(i, h):
+            cols = slice(h * HEAD, (h + 1) * HEAD)
+            v_side = work.tile([P, HEAD, PACK], BF16, align_bytes=64)
+            nc.scalar.copy(out=v_side[:], in_=v_raw[i][:, :, cols].rearrange("p t d -> p d t"))
+            v_grouped[(i, h)] = v_side
+
+        def quantise_values(i, h):
+            nc.vector.quantize_mx(
+                out=v_codes[i][:, h, :].bitcast(FP8X4),
+                scales=v_scales[i][:, h, :],
+                in_=v_grouped[(i, h)][:].rearrange("p d t -> p (d t)"),
+            )
+
+        def score(s):
+            i, h, cells = rounds[s]
+            banks[s] = []
+            for r, j in cells:
+                cell = psum_cell.tile([P, PACK, P], F32)
+                for t in range(PACK):
+                    nc.tensor.matmul(
+                        out=cell[:, t, :],
+                        lhsT=keys_t[j][:, h, t, :],
+                        rhs=queries_t[(i, h)][:, r, :],
+                        start=True,
+                        stop=True,
+                    )
+                banks[s].append(cell)
+
+        def apply_decay(s):
+            i, h, cells = rounds[s]
+            side = work.tile([P, CELLS, P, PACK], BF16, bufs=LAG + 2, align_bytes=64)
+            for e, (r, j) in enumerate(cells):
+                if j == i:
+                    first_plane, factor = PACK - r, 1.0
+                else:
+                    first_plane, factor = 0, gammas[h] ** (SPAN * (i - j - 1) + P * r)
+                table = decay[h][:, :, first_plane : first_plane + PACK]
+                by_query = banks[s][e][:].rearrange("p t x -> p x t")
+                if (CELLS * s + e) % THIRD == THIRD - 1:
+                    scaled = work.tile([P, P, PACK], F32)
+                    nc.scalar.mul(out=scaled[:], in_=by_query, mul=factor)
+                    nc.gpsimd.tensor_tensor(out=side[:, e], in0=scaled[:], in1=table, op=ALU.mult)
+                else:
+                    nc.vector.scalar_tensor_tensor(
+                        out=side[:, e], in0=by_query, scalar=factor, in1=table, op0=ALU.mult, op1=ALU.mult
+                    )
+            grouped[s] = side
+
+        def quantise(s):
+            words = work.tile([P, CELLS, P], U32, align_bytes=64)
+            plane = work.tile([P, CELLS, P], U8, align_bytes=64)
+            nc.vector.quantize_mx(
+                out=words[:].rearrange("p e x -> p (e x)").bitcast(FP8X4),
+                scales=plane[:].rearrange("p e x -> p (e x)"),
+                in_=grouped[s][:].rearrange("p e x t -> p (e x t)"),
+            )
+            codes[s], scales[s] = words, plane
+
+        def multiply(s):
+            i, h, cells = rounds[s]
+            for e, (r, j) in enumerate(cells):
+                if (r, j) == (0, 0):
+                    product = psum_out.tile([P, PACK, HEAD], F32)
+                    products[(i, h)] = product
+                nc.tensor.matmul_mx(
+                    out=products[(i, h)][:, r, :],
+                    lhsT=codes[s][:, e, :].bitcast(FP8X4),
+                    lhsT_scale=scales[s][:, e, :],
+                    rhs=v_codes[j][:, h, :].bitcast(FP8X4),
+                    rhs_scale=v_scales[j][:, h, :],
+                    start=(j == 0),
+                    stop=(j == i),
+                )
+                if (r, j) == (PACK - 1, i):
+                    result = work.tile([P, PACK, HEAD], F32)
+                    nc.scalar.copy(out=result[:], in_=products[(i, h)][:])
+                    nc.sync.dma_start(
+                        out=out_rows[i * SPAN : (i + 1) * SPAN, h * HEAD : (h + 1) * HEAD].rearrange(
+                            "(r p) d -> p r d", p=P
+                        ),
+                        in_=result[:],
+                    )
+
+        load_span(0)
+        load_span(1)
+        prepare(0, 0)
+
+        for s in range(len(rounds) + LAG + 1):
+            starts_job = s < len(rounds) and rounds[s][2][0] == (0, 0)
+            if starts_job:
+                i, h = rounds[s][0], rounds[s][1]
+                if h == 0 and 1 <= i < N_SPANS - 1:
+                    load_span(i + 1)
+                regroup_values(i, h)
+                following = jobs.index((i, h)) + 1
+                if following < len(jobs):
+                    prepare(jobs[following][0], jobs[following][1])
+            if s < len(rounds):
+                score(s)
+            if 0 <= s - LAG - 1:
+                multiply(s - LAG - 1)
+            if s < len(rounds):
+                apply_decay(s)
+            if starts_job:
+                quantise_values(rounds[s][0], rounds[s][1])
+            if 0 <= s - LAG < len(rounds):
+                quantise(s - LAG)

@@ -22,7 +22,7 @@ SPAN = P * PACK
 N_SPANS = SEQ // SPAN
 PLANES = 2 * PACK
 CELLS = 4
-THIRD = 3
+DETOUR = 5
 LAG = 2
 FAR = 1.0e6
 
@@ -136,7 +136,7 @@ def tile_multiscaleretention_pa_kernel(tc, q, k, v, out):
                     first_plane, factor = 0, gammas[h] ** (SPAN * (i - j - 1) + P * r)
                 table = decay[h][:, :, first_plane : first_plane + PACK]
                 by_query = banks[s][e][:].rearrange("p t x -> p x t")
-                if (CELLS * s + e) % THIRD == THIRD - 1:
+                if (CELLS * s + e) % DETOUR == DETOUR - 1:
                     scaled = work.tile([P, P, PACK], F32)
                     nc.scalar.mul(out=scaled[:], in_=by_query, mul=factor)
                     nc.gpsimd.tensor_tensor(out=side[:, e], in0=scaled[:], in1=table, op=ALU.mult)

@@ -22,8 +22,8 @@ SPAN = P * PACK
 N_SPANS = SEQ // SPAN
 PLANES = 2 * PACK
 CELLS = 4
-DETOUR = 5
-LAG = 2
+AHEAD = 2
+LAG = 1
 FAR = 1.0e6
 
 FLOPS = 2 * 2 * HEAD * HEADS * SPAN * SPAN * (1 + 2 + 3 + 4)
@@ -68,7 +68,7 @@ def tile_multiscaleretention_pa_kernel(tc, q, k, v, out):
         keys_t, v_codes, v_scales = {}, {}, {}
         decay = {}
         queries_t, v_grouped, products = {}, {}, {}
-        banks, grouped, codes, scales = {}, {}, {}, {}
+        banks, scaled, grouped, codes, scales = {}, {}, {}, {}, {}
 
         def load_span(i):
             rows = slice(i * SPAN, (i + 1) * SPAN)
@@ -94,7 +94,7 @@ def tile_multiscaleretention_pa_kernel(tc, q, k, v, out):
             for t in range(PACK):
                 nc.tensor.transpose(flipped[:, PACK + t, :], q_raw[i][:, t, cols], identity[:])
             nc.scalar.copy(out=keys_t[i][:, h], in_=flipped[:, 0:PACK, :])
-            q_t = work.tile([P, PACK, P], BF16)
+            q_t = work.tile([P, PACK, P], BF16, bufs=AHEAD + 2)
             nc.scalar.copy(out=q_t[:], in_=flipped[:, PACK : 2 * PACK, :])
             queries_t[(i, h)] = q_t
 
@@ -111,6 +111,13 @@ def tile_multiscaleretention_pa_kernel(tc, q, k, v, out):
                 in_=v_grouped[(i, h)][:].rearrange("p d t -> p (d t)"),
             )
 
+        def decay_of(i, h, r, j):
+            if j == i:
+                first_plane, factor = PACK - r, 1.0
+            else:
+                first_plane, factor = 0, gammas[h] ** (SPAN * (i - j - 1) + P * r)
+            return factor, decay[h][:, :, first_plane : first_plane + PACK]
+
         def score(s):
             i, h, cells = rounds[s]
             banks[s] = []
@@ -125,28 +132,32 @@ def tile_multiscaleretention_pa_kernel(tc, q, k, v, out):
                         stop=True,
                     )
                 banks[s].append(cell)
+            factor = decay_of(i, h, cells[0][0], cells[0][1])[0]
+            first_out = work.tile([P, P, PACK], F32)
+            nc.scalar.mul(out=first_out[:], in_=banks[s][0][:].rearrange("p t x -> p x t"), mul=factor)
+            scaled[s] = first_out
 
         def apply_decay(s):
             i, h, cells = rounds[s]
-            side = work.tile([P, CELLS, P, PACK], BF16, bufs=LAG + 2, align_bytes=64)
+            side = work.tile([P, CELLS, P, PACK], BF16, bufs=LAG + 1, align_bytes=64)
             for e, (r, j) in enumerate(cells):
-                if j == i:
-                    first_plane, factor = PACK - r, 1.0
-                else:
-                    first_plane, factor = 0, gammas[h] ** (SPAN * (i - j - 1) + P * r)
-                table = decay[h][:, :, first_plane : first_plane + PACK]
-                by_query = banks[s][e][:].rearrange("p t x -> p x t")
-                if (CELLS * s + e) % DETOUR == DETOUR - 1:
-                    scaled = work.tile([P, P, PACK], F32)
-                    nc.scalar.mul(out=scaled[:], in_=by_query, mul=factor)
-                    nc.gpsimd.tensor_tensor(out=side[:, e], in0=scaled[:], in1=table, op=ALU.mult)
+                factor, table = decay_of(i, h, r, j)
+                if e == 0:
+                    nc.gpsimd.tensor_tensor(out=side[:, e], in0=scaled[s][:], in1=table, op=ALU.mult)
                 else:
                     nc.vector.scalar_tensor_tensor(
-                        out=side[:, e], in0=by_query, scalar=factor, in1=table, op0=ALU.mult, op1=ALU.mult
+                        out=side[:, e],
+                        in0=banks[s][e][:].rearrange("p t x -> p x t"),
+                        scalar=factor,
+                        in1=table,
+                        op0=ALU.mult,
+                        op1=ALU.mult,
                     )
             grouped[s] = side
 
         def quantise(s):
+            if rounds[s][2][0] == (0, 0):
+                quantise_values(rounds[s][0], rounds[s][1])
             words = work.tile([P, CELLS, P], U32, align_bytes=64)
             plane = work.tile([P, CELLS, P], U8, align_bytes=64)
             nc.vector.quantize_mx(
@@ -183,25 +194,22 @@ def tile_multiscaleretention_pa_kernel(tc, q, k, v, out):
 
         load_span(0)
         load_span(1)
-        prepare(0, 0)
+        for i, h in jobs[0:AHEAD]:
+            prepare(i, h)
 
         for s in range(len(rounds) + LAG + 1):
-            starts_job = s < len(rounds) and rounds[s][2][0] == (0, 0)
-            if starts_job:
-                i, h = rounds[s][0], rounds[s][1]
-                if h == 0 and 1 <= i < N_SPANS - 1:
-                    load_span(i + 1)
-                regroup_values(i, h)
-                following = jobs.index((i, h)) + 1
-                if following < len(jobs):
-                    prepare(jobs[following][0], jobs[following][1])
             if s < len(rounds):
                 score(s)
+                i, h, cells = rounds[s]
+                if cells[0] == (0, 0):
+                    if h == 0 and 1 <= i < N_SPANS - 1:
+                        load_span(i + 1)
+                    regroup_values(i, h)
+                    for later in jobs[jobs.index((i, h)) + AHEAD : jobs.index((i, h)) + AHEAD + 1]:
+                        prepare(later[0], later[1])
             if 0 <= s - LAG - 1:
                 multiply(s - LAG - 1)
             if s < len(rounds):
                 apply_decay(s)
-            if starts_job:
-                quantise_values(rounds[s][0], rounds[s][1])
             if 0 <= s - LAG < len(rounds):
                 quantise(s - LAG)

@@ -20,10 +20,10 @@ P = 128
 PACK = 4
 SPAN = P * PACK
 N_SPANS = SEQ // SPAN
-PLANES = 2 * PACK
 CELLS = 4
+LOAD_HEADS = 4
 AHEAD = 2
-LAG = 1
+LAG = 2
 FAR = 1.0e6
 
 FLOPS = 2 * 2 * HEAD * HEADS * SPAN * SPAN * (1 + 2 + 3 + 4)
@@ -40,90 +40,96 @@ def tile_multiscaleretention_pa_kernel(tc, q, k, v, out):
     jobs = [(i, h) for i in range(N_SPANS) for h in range(HEADS)]
     rounds = []
     for i, h in jobs:
-        cells = [(r, j) for r in range(PACK) for j in range(i + 1)]
-        for first in range(0, len(cells), CELLS):
-            rounds.append((i, h, cells[first : first + CELLS]))
+        rounds.append((i, h, [(r, i) for r in range(PACK)]))
+        below = [(r, j) for r in range(PACK) for j in range(i)]
+        for first in range(0, len(below), CELLS):
+            rounds.append((i, h, below[first : first + CELLS]))
 
     with ExitStack() as stack:
         keep = stack.enter_context(tc.tile_pool(name="keep", bufs=1))
-        raw = stack.enter_context(tc.tile_pool(name="raw", bufs=2))
+        raw = stack.enter_context(tc.tile_pool(name="raw", bufs=2 * HEADS // LOAD_HEADS))
         work = stack.enter_context(tc.tile_pool(name="work", bufs=3))
         psum_flip = stack.enter_context(tc.psum_pool(name="psum_flip", bufs=2))
         psum_cell = stack.enter_context(tc.psum_pool(name="psum_cell", bufs=CELLS))
         psum_out = stack.enter_context(tc.psum_pool(name="psum_out", bufs=2))
         stack.enter_context(tc.manual_schedule())
 
+        steps_int = keep.tile([P, PACK + 1, P], I32)
+        nc.gpsimd.iota(out=steps_int[:], pattern=[[-P, PACK + 1], [1, P]], base=PACK * P, channel_multiplier=-1)
+        steps = keep.tile([P, PACK + 1, P], F32)
+        nc.vector.tensor_copy(out=steps[:], in_=steps_int[:])
+        push = keep.tile([P, P], F32)
+        nc.vector.tensor_scalar(
+            out=push[:], in0=steps[:, PACK, :], scalar1=0.0, scalar2=FAR, op0=ALU.is_lt, op1=ALU.mult
+        )
+        nc.vector.tensor_tensor(out=steps[:, PACK, :], in0=steps[:, PACK, :], in1=push[:], op=ALU.add)
+
         identity = keep.tile([P, P], BF16)
         make_identity(nc, identity[:])
 
-        steps_int = keep.tile([P, P, PLANES], I32)
-        nc.gpsimd.iota(out=steps_int[:], pattern=[[1, P], [-P, PLANES]], base=PACK * P, channel_multiplier=-1)
-        steps = keep.tile([P, P, PLANES], F32)
-        nc.vector.tensor_copy(out=steps[:], in_=steps_int[:])
-        push = keep.tile([P, P, PLANES], F32)
-        nc.vector.tensor_scalar(out=push[:], in0=steps[:], scalar1=0.0, scalar2=FAR, op0=ALU.is_lt, op1=ALU.mult)
-        nc.vector.tensor_tensor(out=steps[:], in0=steps[:], in1=push[:], op=ALU.add)
+        diagonal_side = []
+        for turn in range(LAG + 1):
+            zeroed = keep.tile([P, CELLS, P, PACK], BF16, name="diagonal_side%d" % turn, align_bytes=64)
+            nc.vector.memset(zeroed[:], 0.0)
+            diagonal_side.append(zeroed)
 
         q_raw, k_raw, v_raw = {}, {}, {}
         keys_t, v_codes, v_scales = {}, {}, {}
         decay = {}
-        queries_t, v_grouped, products = {}, {}, {}
+        queries_t, v_grouped, products, opening = {}, {}, {}, {}
         banks, scaled, grouped, codes, scales = {}, {}, {}, {}, {}
 
         def load_span(i):
             rows = slice(i * SPAN, (i + 1) * SPAN)
-            k_in = raw.tile([P, PACK, HEADS * HEAD], BF16)
-            nc.sync.dma_start(out=k_in[:], in_=k_rows[rows, :].rearrange("(t p) c -> p t c", p=P))
-            q_in = raw.tile([P, PACK, HEADS * HEAD], BF16)
-            nc.sync.dma_start(out=q_in[:], in_=q_rows[rows, :].rearrange("(t p) c -> p t c", p=P))
-            v_in = raw.tile([P, PACK, HEADS * HEAD], BF16)
-            nc.sync.dma_start(out=v_in[:], in_=v_rows[rows, :].rearrange("(t p) c -> p t c", p=P))
-            k_raw[i], q_raw[i], v_raw[i] = k_in, q_in, v_in
+            for part in range(HEADS // LOAD_HEADS):
+                cols = slice(part * LOAD_HEADS * HEAD, (part + 1) * LOAD_HEADS * HEAD)
+                k_in = raw.tile([P, PACK, LOAD_HEADS * HEAD], BF16)
+                nc.sync.dma_start(out=k_in[:], in_=k_rows[rows, cols].rearrange("(t p) c -> p t c", p=P))
+                q_in = raw.tile([P, PACK, LOAD_HEADS * HEAD], BF16)
+                nc.sync.dma_start(out=q_in[:], in_=q_rows[rows, cols].rearrange("(t p) c -> p t c", p=P))
+                v_in = raw.tile([P, PACK, LOAD_HEADS * HEAD], BF16)
+                nc.sync.dma_start(out=v_in[:], in_=v_rows[rows, cols].rearrange("(t p) c -> p t c", p=P))
+                k_raw[(i, part)], q_raw[(i, part)], v_raw[(i, part)] = k_in, q_in, v_in
             keys_t[i] = keep.tile([P, HEADS, PACK, P], BF16, name="keys_t%d" % i)
             v_codes[i] = keep.tile([P, HEADS, HEAD], U32, name="v_codes%d" % i, align_bytes=64)
             v_scales[i] = keep.tile([P, HEADS, HEAD], U8, name="v_scales%d" % i, align_bytes=64)
 
+        def loaded(tiles, i, h):
+            first = (h % LOAD_HEADS) * HEAD
+            return tiles[(i, h // LOAD_HEADS)][:, :, first : first + HEAD]
+
         def prepare(i, h):
-            cols = slice(h * HEAD, (h + 1) * HEAD)
             if i == 0:
-                decay[h] = keep.tile([P, P, PLANES], F32, name="decay%d" % h)
+                decay[h] = keep.tile([P, PACK + 1, P], F32, name="decay%d" % h)
                 nc.scalar.activation(out=decay[h][:], in_=steps[:], func=ACT.Exp, scale=math.log(gammas[h]))
             flipped = psum_flip.tile([P, 2 * PACK, P], BF16)
             for t in range(PACK):
-                nc.tensor.transpose(flipped[:, t, :], k_raw[i][:, t, cols], identity[:])
+                nc.tensor.transpose(flipped[:, t, :], loaded(k_raw, i, h)[:, t, :], identity[:])
             for t in range(PACK):
-                nc.tensor.transpose(flipped[:, PACK + t, :], q_raw[i][:, t, cols], identity[:])
+                nc.tensor.transpose(flipped[:, PACK + t, :], loaded(q_raw, i, h)[:, t, :], identity[:])
             nc.scalar.copy(out=keys_t[i][:, h], in_=flipped[:, 0:PACK, :])
             q_t = work.tile([P, PACK, P], BF16, bufs=AHEAD + 2)
             nc.scalar.copy(out=q_t[:], in_=flipped[:, PACK : 2 * PACK, :])
             queries_t[(i, h)] = q_t
 
         def regroup_values(i, h):
-            cols = slice(h * HEAD, (h + 1) * HEAD)
-            v_side = work.tile([P, HEAD, PACK], BF16, align_bytes=64)
-            nc.scalar.copy(out=v_side[:], in_=v_raw[i][:, :, cols].rearrange("p t d -> p d t"))
+            v_side = work.tile([P, HEAD, PACK], BF16, bufs=LAG + 2, align_bytes=64)
+            nc.scalar.copy(out=v_side[:], in_=loaded(v_raw, i, h).rearrange("p t d -> p d t"))
             v_grouped[(i, h)] = v_side
-
-        def quantise_values(i, h):
-            nc.vector.quantize_mx(
-                out=v_codes[i][:, h, :].bitcast(FP8X4),
-                scales=v_scales[i][:, h, :],
-                in_=v_grouped[(i, h)][:].rearrange("p d t -> p (d t)"),
-            )
 
         def decay_of(i, h, r, j):
             if j == i:
-                first_plane, factor = PACK - r, 1.0
+                strips, first_plane, factor = r + 1, PACK - r, 1.0
             else:
-                first_plane, factor = 0, gammas[h] ** (SPAN * (i - j - 1) + P * r)
-            return factor, decay[h][:, :, first_plane : first_plane + PACK]
+                strips, first_plane, factor = PACK, 0, gammas[h] ** (SPAN * (i - j - 1) + P * r)
+            return strips, factor, decay[h][:, first_plane : first_plane + strips, :].rearrange("p t x -> p x t")
 
         def score(s):
             i, h, cells = rounds[s]
             banks[s] = []
             for r, j in cells:
                 cell = psum_cell.tile([P, PACK, P], F32)
-                for t in range(PACK):
+                for t in range(decay_of(i, h, r, j)[0]):
                     nc.tensor.matmul(
                         out=cell[:, t, :],
                         lhsT=keys_t[j][:, h, t, :],
@@ -132,22 +138,29 @@ def tile_multiscaleretention_pa_kernel(tc, q, k, v, out):
                         stop=True,
                     )
                 banks[s].append(cell)
-            factor = decay_of(i, h, cells[0][0], cells[0][1])[0]
-            first_out = work.tile([P, P, PACK], F32)
-            nc.scalar.mul(out=first_out[:], in_=banks[s][0][:].rearrange("p t x -> p x t"), mul=factor)
-            scaled[s] = first_out
+            if cells[0][1] < i:
+                first_out = work.tile([P, P, PACK], F32)
+                nc.scalar.mul(
+                    out=first_out[:],
+                    in_=banks[s][0][:].rearrange("p t x -> p x t"),
+                    mul=decay_of(i, h, cells[0][0], cells[0][1])[1],
+                )
+                scaled[s] = first_out
 
         def apply_decay(s):
             i, h, cells = rounds[s]
-            side = work.tile([P, CELLS, P, PACK], BF16, bufs=LAG + 1, align_bytes=64)
+            if cells[0][1] == i:
+                side = diagonal_side[jobs.index((i, h)) % (LAG + 1)]
+            else:
+                side = work.tile([P, CELLS, P, PACK], BF16, bufs=LAG + 2, align_bytes=64)
             for e, (r, j) in enumerate(cells):
-                factor, table = decay_of(i, h, r, j)
-                if e == 0:
+                strips, factor, table = decay_of(i, h, r, j)
+                if e == 0 and j < i:
                     nc.gpsimd.tensor_tensor(out=side[:, e], in0=scaled[s][:], in1=table, op=ALU.mult)
                 else:
                     nc.vector.scalar_tensor_tensor(
-                        out=side[:, e],
-                        in0=banks[s][e][:].rearrange("p t x -> p x t"),
+                        out=side[:, e, :, 0:strips],
+                        in0=banks[s][e][:, 0:strips, :].rearrange("p t x -> p x t"),
                         scalar=factor,
                         in1=table,
                         op0=ALU.mult,
@@ -156,10 +169,19 @@ def tile_multiscaleretention_pa_kernel(tc, q, k, v, out):
             grouped[s] = side
 
         def quantise(s):
-            if rounds[s][2][0] == (0, 0):
-                quantise_values(rounds[s][0], rounds[s][1])
-            words = work.tile([P, CELLS, P], U32, align_bytes=64)
-            plane = work.tile([P, CELLS, P], U8, align_bytes=64)
+            i, h, cells = rounds[s]
+            if cells[0][1] == i:
+                nc.vector.quantize_mx(
+                    out=v_codes[i][:, h, :].bitcast(FP8X4),
+                    scales=v_scales[i][:, h, :],
+                    in_=v_grouped[(i, h)][:].rearrange("p d t -> p (d t)"),
+                )
+                words = work.tile([P, CELLS, P], U32, name="diagonal_words", bufs=2, align_bytes=64)
+                plane = work.tile([P, CELLS, P], U8, name="diagonal_plane", bufs=2, align_bytes=64)
+                opening[(i, h)] = s
+            else:
+                words = work.tile([P, CELLS, P], U32, align_bytes=64)
+                plane = work.tile([P, CELLS, P], U8, align_bytes=64)
             nc.vector.quantize_mx(
                 out=words[:].rearrange("p e x -> p (e x)").bitcast(FP8X4),
                 scales=plane[:].rearrange("p e x -> p (e x)"),
@@ -167,30 +189,38 @@ def tile_multiscaleretention_pa_kernel(tc, q, k, v, out):
             )
             codes[s], scales[s] = words, plane
 
+        def mx_pass(i, h, r, j, s, e, start, stop):
+            nc.tensor.matmul_mx(
+                out=products[(i, h)][:, r, :],
+                lhsT=codes[s][:, e, :].bitcast(FP8X4),
+                lhsT_scale=scales[s][:, e, :],
+                rhs=v_codes[j][:, h, :].bitcast(FP8X4),
+                rhs_scale=v_scales[j][:, h, :],
+                start=start,
+                stop=stop,
+            )
+
         def multiply(s):
             i, h, cells = rounds[s]
+            if cells[0] == (0, i):
+                product = psum_out.tile([P, PACK, HEAD], F32)
+                products[(i, h)] = product
             for e, (r, j) in enumerate(cells):
-                if (r, j) == (0, 0):
-                    product = psum_out.tile([P, PACK, HEAD], F32)
-                    products[(i, h)] = product
-                nc.tensor.matmul_mx(
-                    out=products[(i, h)][:, r, :],
-                    lhsT=codes[s][:, e, :].bitcast(FP8X4),
-                    lhsT_scale=scales[s][:, e, :],
-                    rhs=v_codes[j][:, h, :].bitcast(FP8X4),
-                    rhs_scale=v_scales[j][:, h, :],
-                    start=(j == 0),
-                    stop=(j == i),
+                if i == 0:
+                    mx_pass(i, h, r, j, s, e, True, True)
+                elif j < i:
+                    if j == 0:
+                        mx_pass(i, h, r, i, opening[(i, h)], r, True, False)
+                    mx_pass(i, h, r, j, s, e, False, j == i - 1)
+            if cells[-1] == (PACK - 1, max(i - 1, 0)):
+                result = work.tile([P, PACK, HEAD], F32)
+                nc.scalar.copy(out=result[:], in_=products[(i, h)][:])
+                nc.sync.dma_start(
+                    out=out_rows[i * SPAN : (i + 1) * SPAN, h * HEAD : (h + 1) * HEAD].rearrange(
+                        "(r p) d -> p r d", p=P
+                    ),
+                    in_=result[:],
                 )
-                if (r, j) == (PACK - 1, i):
-                    result = work.tile([P, PACK, HEAD], F32)
-                    nc.scalar.copy(out=result[:], in_=products[(i, h)][:])
-                    nc.sync.dma_start(
-                        out=out_rows[i * SPAN : (i + 1) * SPAN, h * HEAD : (h + 1) * HEAD].rearrange(
-                            "(r p) d -> p r d", p=P
-                        ),
-                        in_=result[:],
-                    )
 
         load_span(0)
         load_span(1)
@@ -201,7 +231,7 @@ def tile_multiscaleretention_pa_kernel(tc, q, k, v, out):
             if s < len(rounds):
                 score(s)
                 i, h, cells = rounds[s]
-                if cells[0] == (0, 0):
+                if cells[0] == (0, i):
                     if h == 0 and 1 <= i < N_SPANS - 1:
                         load_span(i + 1)
                     regroup_values(i, h)

@@ -54,15 +54,15 @@ def tile_multiscaleretention_pa_kernel(tc, q, k, v, out):
         psum_out = stack.enter_context(tc.psum_pool(name="psum_out", bufs=2))
         stack.enter_context(tc.manual_schedule())
 
-        steps_int = keep.tile([P, PACK + 1, P], I32)
-        nc.gpsimd.iota(out=steps_int[:], pattern=[[-P, PACK + 1], [1, P]], base=PACK * P, channel_multiplier=-1)
-        steps = keep.tile([P, PACK + 1, P], F32)
-        nc.vector.tensor_copy(out=steps[:], in_=steps_int[:])
-        push = keep.tile([P, P], F32)
-        nc.vector.tensor_scalar(
-            out=push[:], in0=steps[:, PACK, :], scalar1=0.0, scalar2=FAR, op0=ALU.is_lt, op1=ALU.mult
+        steps_int = keep.tile([P, 2, P, PACK], I32)
+        nc.gpsimd.iota(
+            out=steps_int[:], pattern=[[-P, 2], [1, P], [-P, PACK]], base=PACK * P, channel_multiplier=-1
         )
-        nc.vector.tensor_tensor(out=steps[:, PACK, :], in0=steps[:, PACK, :], in1=push[:], op=ALU.add)
+        steps = keep.tile([P, 2, P, PACK], F32)
+        nc.vector.tensor_copy(out=steps[:], in_=steps_int[:])
+        push = keep.tile([P, 2, P, PACK], F32)
+        nc.vector.tensor_scalar(out=push[:], in0=steps[:], scalar1=0.0, scalar2=FAR, op0=ALU.is_lt, op1=ALU.mult)
+        nc.vector.tensor_tensor(out=steps[:], in0=steps[:], in1=push[:], op=ALU.add)
 
         identity = keep.tile([P, P], BF16)
         make_identity(nc, identity[:])
@@ -100,7 +100,7 @@ def tile_multiscaleretention_pa_kernel(tc, q, k, v, out):
 
         def prepare(i, h):
             if i == 0:
-                decay[h] = keep.tile([P, PACK + 1, P], F32, name="decay%d" % h)
+                decay[h] = keep.tile([P, 2, P, PACK], F32, name="decay%d" % h)
                 nc.scalar.activation(out=decay[h][:], in_=steps[:], func=ACT.Exp, scale=math.log(gammas[h]))
             flipped = psum_flip.tile([P, 2 * PACK, P], BF16)
             for t in range(PACK):
@@ -119,10 +119,8 @@ def tile_multiscaleretention_pa_kernel(tc, q, k, v, out):
 
         def decay_of(i, h, r, j):
             if j == i:
-                strips, first_plane, factor = r + 1, PACK - r, 1.0
-            else:
-                strips, first_plane, factor = PACK, 0, gammas[h] ** (SPAN * (i - j - 1) + P * r)
-            return strips, factor, decay[h][:, first_plane : first_plane + strips, :].rearrange("p t x -> p x t")
+                return r + 1, 1.0, decay[h][:, 1, :, PACK - 1 - r : PACK]
+            return PACK, gammas[h] ** (SPAN * (i - j - 1) + P * r), decay[h][:, 0, :, :]
 
         def score(s):
             i, h, cells = rounds[s]

@@ -23,6 +23,7 @@ N_SPANS = SEQ // SPAN
 CELLS = 4
 LOAD_HEADS = 4
 AHEAD = 2
+SHORT_DETOURS = 2
 LAG = 2
 FAR = 1.0e6
 
@@ -75,9 +76,10 @@ def tile_multiscaleretention_pa_kernel(tc, q, k, v, out):
 
         q_raw, k_raw, v_raw = {}, {}, {}
         keys_t, v_codes, v_scales = {}, {}, {}
-        decay = {}
+        decay_below, decay_diagonal = {}, {}
         queries_t, v_grouped, products, opening = {}, {}, {}, {}
-        banks, scaled, grouped, codes, scales = {}, {}, {}, {}, {}
+        banks, grouped, codes, scales = {}, {}, {}, {}
+        scaled = {}
 
         def load_span(i):
             rows = slice(i * SPAN, (i + 1) * SPAN)
@@ -100,8 +102,13 @@ def tile_multiscaleretention_pa_kernel(tc, q, k, v, out):
 
         def prepare(i, h):
             if i == 0:
-                decay[h] = keep.tile([P, 2, P, PACK], F32, name="decay%d" % h)
-                nc.scalar.activation(out=decay[h][:], in_=steps[:], func=ACT.Exp, scale=math.log(gammas[h]))
+                decay_diagonal[h] = keep.tile([P, P, PACK], F32, name="decay_diagonal%d" % h)
+                nc.scalar.activation(
+                    out=decay_diagonal[h][:], in_=steps[:, 1], func=ACT.Exp, scale=math.log(gammas[h])
+                )
+            if i == 1:
+                decay_below[h] = keep.tile([P, P, PACK], F32, name="decay_below%d" % h)
+                nc.scalar.activation(out=decay_below[h][:], in_=steps[:, 0], func=ACT.Exp, scale=math.log(gammas[h]))
             flipped = psum_flip.tile([P, 2 * PACK, P], BF16)
             for t in range(PACK):
                 nc.tensor.transpose(flipped[:, t, :], loaded(k_raw, i, h)[:, t, :], identity[:])
@@ -119,15 +126,21 @@ def tile_multiscaleretention_pa_kernel(tc, q, k, v, out):
 
         def decay_of(i, h, r, j):
             if j == i:
-                return r + 1, 1.0, decay[h][:, 1, :, PACK - 1 - r : PACK]
-            return PACK, gammas[h] ** (SPAN * (i - j - 1) + P * r), decay[h][:, 0, :, :]
+                return r + 1, 1.0, decay_diagonal[h][:, :, PACK - 1 - r : PACK]
+            return PACK, gammas[h] ** (SPAN * (i - j - 1) + P * r), decay_below[h][:]
+
+        def makes_detour(i, e, r, j):
+            if j == i:
+                return r < SHORT_DETOURS
+            return e == 0
 
         def score(s):
             i, h, cells = rounds[s]
             banks[s] = []
-            for r, j in cells:
+            for e, (r, j) in enumerate(cells):
+                strips, factor, table = decay_of(i, h, r, j)
                 cell = psum_cell.tile([P, PACK, P], F32)
-                for t in range(decay_of(i, h, r, j)[0]):
+                for t in range(strips):
                     nc.tensor.matmul(
                         out=cell[:, t, :],
                         lhsT=keys_t[j][:, h, t, :],
@@ -136,14 +149,10 @@ def tile_multiscaleretention_pa_kernel(tc, q, k, v, out):
                         stop=True,
                     )
                 banks[s].append(cell)
-            if cells[0][1] < i:
-                first_out = work.tile([P, P, PACK], F32)
-                nc.scalar.mul(
-                    out=first_out[:],
-                    in_=banks[s][0][:].rearrange("p t x -> p x t"),
-                    mul=decay_of(i, h, cells[0][0], cells[0][1])[1],
-                )
-                scaled[s] = first_out
+                if makes_detour(i, e, r, j):
+                    taken_out = work.tile([P, P, strips], F32, bufs=4)
+                    nc.scalar.mul(out=taken_out[:], in_=cell[:, 0:strips, :].rearrange("p t x -> p x t"), mul=factor)
+                    scaled[(s, e)] = taken_out
 
         def apply_decay(s):
             i, h, cells = rounds[s]
@@ -153,8 +162,8 @@ def tile_multiscaleretention_pa_kernel(tc, q, k, v, out):
                 side = work.tile([P, CELLS, P, PACK], BF16, bufs=LAG + 2, align_bytes=64)
             for e, (r, j) in enumerate(cells):
                 strips, factor, table = decay_of(i, h, r, j)
-                if e == 0 and j < i:
-                    nc.gpsimd.tensor_tensor(out=side[:, e], in0=scaled[s][:], in1=table, op=ALU.mult)
+                if makes_detour(i, e, r, j):
+                    nc.gpsimd.tensor_tensor(out=side[:, e, :, 0:strips], in0=scaled[(s, e)][:], in1=table, op=ALU.mult)
                 else:
                     nc.vector.scalar_tensor_tensor(
                         out=side[:, e, :, 0:strips],

@@ -55,24 +55,28 @@ def tile_multiscaleretention_pa_kernel(tc, q, k, v, out):
         psum_out = stack.enter_context(tc.psum_pool(name="psum_out", bufs=2))
         stack.enter_context(tc.manual_schedule())
 
-        steps_int = keep.tile([P, 2, P, PACK], I32)
-        nc.gpsimd.iota(
-            out=steps_int[:], pattern=[[-P, 2], [1, P], [-P, PACK]], base=PACK * P, channel_multiplier=-1
-        )
-        steps = keep.tile([P, 2, P, PACK], F32)
-        nc.vector.tensor_copy(out=steps[:], in_=steps_int[:])
-        push = keep.tile([P, 2, P, PACK], F32)
-        nc.vector.tensor_scalar(out=push[:], in0=steps[:], scalar1=0.0, scalar2=FAR, op0=ALU.is_lt, op1=ALU.mult)
-        nc.vector.tensor_tensor(out=steps[:], in0=steps[:], in1=push[:], op=ALU.add)
-
-        identity = keep.tile([P, P], BF16)
-        make_identity(nc, identity[:])
-
         diagonal_side = []
         for turn in range(LAG + 1):
             zeroed = keep.tile([P, CELLS, P, PACK], BF16, name="diagonal_side%d" % turn, align_bytes=64)
-            nc.vector.memset(zeroed[:], 0.0)
+            nc.vector.memset(zeroed[:].rearrange("p e x t -> p (e x t)").bitcast(I32), 0)
             diagonal_side.append(zeroed)
+
+        steps_int = keep.tile([P, 2, P, PACK], I32)
+        steps_diagonal = keep.tile([P, P, PACK], F32)
+        steps_below = keep.tile([P, P, PACK], F32)
+        push = keep.tile([P, P, PACK], F32)
+        identity = keep.tile([P, P], BF16)
+        nc.gpsimd.iota(
+            out=steps_int[:, 0], pattern=[[1, P], [-P, PACK]], base=(PACK - 1) * P, channel_multiplier=-1
+        )
+        nc.vector.tensor_copy(out=steps_diagonal[:], in_=steps_int[:, 0])
+        nc.vector.tensor_scalar(
+            out=push[:], in0=steps_diagonal[:], scalar1=0.0, scalar2=FAR, op0=ALU.is_lt, op1=ALU.mult
+        )
+        nc.vector.tensor_tensor(out=steps_diagonal[:], in0=steps_diagonal[:], in1=push[:], op=ALU.add)
+        make_identity(nc, identity[:])
+        nc.gpsimd.iota(out=steps_int[:, 1], pattern=[[1, P], [-P, PACK]], base=PACK * P, channel_multiplier=-1)
+        nc.vector.tensor_copy(out=steps_below[:], in_=steps_int[:, 1])
 
         q_raw, k_raw, v_raw = {}, {}, {}
         keys_t, v_codes, v_scales = {}, {}, {}
@@ -104,11 +108,11 @@ def tile_multiscaleretention_pa_kernel(tc, q, k, v, out):
             if i == 0:
                 decay_diagonal[h] = keep.tile([P, P, PACK], F32, name="decay_diagonal%d" % h)
                 nc.scalar.activation(
-                    out=decay_diagonal[h][:], in_=steps[:, 1], func=ACT.Exp, scale=math.log(gammas[h])
+                    out=decay_diagonal[h][:], in_=steps_diagonal[:], func=ACT.Exp, scale=math.log(gammas[h])
                 )
             if i == 1:
                 decay_below[h] = keep.tile([P, P, PACK], F32, name="decay_below%d" % h)
-                nc.scalar.activation(out=decay_below[h][:], in_=steps[:, 0], func=ACT.Exp, scale=math.log(gammas[h]))
+                nc.scalar.activation(out=decay_below[h][:], in_=steps_below[:], func=ACT.Exp, scale=math.log(gammas[h]))
             flipped = psum_flip.tile([P, 2 * PACK, P], BF16)
             for t in range(PACK):
                 nc.tensor.transpose(flipped[:, t, :], loaded(k_raw, i, h)[:, t, :], identity[:])

@@ -163,7 +163,7 @@ def tile_multiscaleretention_pa_kernel(tc, q, k, v, out):
             if cells[0][1] == i:
                 side = diagonal_side[jobs.index((i, h)) % (LAG + 1)]
             else:
-                side = work.tile([P, CELLS, P, PACK], BF16, bufs=LAG + 2, align_bytes=64)
+                side = work.tile([P, CELLS, P, PACK], BF16, bufs=LAG + 1, align_bytes=64)
             for e, (r, j) in enumerate(cells):
                 strips, factor, table = decay_of(i, h, r, j)
                 if makes_detour(i, e, r, j):

import math
from contextlib import ExitStack

import concourse.mybir as mybir
from concourse.masks import make_identity

BF16 = mybir.dt.bfloat16
F32 = mybir.dt.float32
I32 = mybir.dt.int32
U32 = mybir.dt.uint32
U8 = mybir.dt.uint8
FP8X4 = mybir.dt.float8_e4m3fn_x4
ALU = mybir.AluOpType
ACT = mybir.ActivationFunctionType

SEQ = 2048
HEADS = 8
HEAD = 128
P = 128
PACK = 4
SPAN = P * PACK
N_SPANS = SEQ // SPAN
CELLS = 4
LOAD_HEADS = 4
AHEAD = 2
SHORT_DETOURS = 2
LAG = 2
FAR = 1.0e6

FLOPS = 2 * 2 * HEAD * HEADS * SPAN * SPAN * (1 + 2 + 3 + 4)


def tile_multiscaleretention_pa_kernel(tc, q, k, v, out):
    nc = tc.nc
    q_rows = q.rearrange("b s h d -> (b s) (h d)")
    k_rows = k.rearrange("b s h d -> (b s) (h d)")
    v_rows = v.rearrange("b s h d -> (b s) (h d)")
    out_rows = out.rearrange("b s h d -> (b s) (h d)")
    gammas = [1.0 - 2.0 ** (-9.0 + 4.0 * h / 7.0) for h in range(HEADS)]

    jobs = [(i, h) for i in range(N_SPANS) for h in range(HEADS)]
    rounds = []
    for i, h in jobs:
        rounds.append((i, h, [(r, i) for r in range(PACK)]))
        below = [(r, j) for r in range(PACK) for j in range(i)]
        for first in range(0, len(below), CELLS):
            rounds.append((i, h, below[first : first + CELLS]))

    with ExitStack() as stack:
        keep = stack.enter_context(tc.tile_pool(name="keep", bufs=1))
        raw = stack.enter_context(tc.tile_pool(name="raw", bufs=2 * HEADS // LOAD_HEADS))
        work = stack.enter_context(tc.tile_pool(name="work", bufs=3))
        psum_flip = stack.enter_context(tc.psum_pool(name="psum_flip", bufs=2))
        psum_cell = stack.enter_context(tc.psum_pool(name="psum_cell", bufs=CELLS))
        psum_out = stack.enter_context(tc.psum_pool(name="psum_out", bufs=2))
        stack.enter_context(tc.manual_schedule())

        diagonal_side = []
        for turn in range(LAG + 1):
            zeroed = keep.tile([P, CELLS, P, PACK], BF16, name="diagonal_side%d" % turn, align_bytes=64)
            nc.vector.memset(zeroed[:].rearrange("p e x t -> p (e x t)").bitcast(I32), 0)
            diagonal_side.append(zeroed)

        steps_int = keep.tile([P, 2, P, PACK], I32)
        steps_diagonal = keep.tile([P, P, PACK], F32)
        steps_below = keep.tile([P, P, PACK], F32)
        push = keep.tile([P, P, PACK], F32)
        identity = keep.tile([P, P], BF16)
        nc.gpsimd.iota(
            out=steps_int[:, 0], pattern=[[1, P], [-P, PACK]], base=(PACK - 1) * P, channel_multiplier=-1
        )
        nc.vector.tensor_copy(out=steps_diagonal[:], in_=steps_int[:, 0])
        nc.vector.tensor_scalar(
            out=push[:], in0=steps_diagonal[:], scalar1=0.0, scalar2=FAR, op0=ALU.is_lt, op1=ALU.mult
        )
        nc.vector.tensor_tensor(out=steps_diagonal[:], in0=steps_diagonal[:], in1=push[:], op=ALU.add)
        make_identity(nc, identity[:])
        nc.gpsimd.iota(out=steps_int[:, 1], pattern=[[1, P], [-P, PACK]], base=PACK * P, channel_multiplier=-1)
        nc.vector.tensor_copy(out=steps_below[:], in_=steps_int[:, 1])

        q_raw, k_raw, v_raw = {}, {}, {}
        keys_t, v_codes, v_scales = {}, {}, {}
        decay_below, decay_diagonal = {}, {}
        queries_t, v_grouped, products, opening = {}, {}, {}, {}
        banks, grouped, codes, scales = {}, {}, {}, {}
        scaled = {}

        def load_span(i):
            rows = slice(i * SPAN, (i + 1) * SPAN)
            for part in range(HEADS // LOAD_HEADS):
                cols = slice(part * LOAD_HEADS * HEAD, (part + 1) * LOAD_HEADS * HEAD)
                k_in = raw.tile([P, PACK, LOAD_HEADS * HEAD], BF16)
                nc.sync.dma_start(out=k_in[:], in_=k_rows[rows, cols].rearrange("(t p) c -> p t c", p=P))
                q_in = raw.tile([P, PACK, LOAD_HEADS * HEAD], BF16)
                nc.sync.dma_start(out=q_in[:], in_=q_rows[rows, cols].rearrange("(t p) c -> p t c", p=P))
                v_in = raw.tile([P, PACK, LOAD_HEADS * HEAD], BF16)
                nc.sync.dma_start(out=v_in[:], in_=v_rows[rows, cols].rearrange("(t p) c -> p t c", p=P))
                k_raw[(i, part)], q_raw[(i, part)], v_raw[(i, part)] = k_in, q_in, v_in
            keys_t[i] = keep.tile([P, HEADS, PACK, P], BF16, name="keys_t%d" % i)
            v_codes[i] = keep.tile([P, HEADS, HEAD], U32, name="v_codes%d" % i, align_bytes=64)
            v_scales[i] = keep.tile([P, HEADS, HEAD], U8, name="v_scales%d" % i, align_bytes=64)

        def loaded(tiles, i, h):
            first = (h % LOAD_HEADS) * HEAD
            return tiles[(i, h // LOAD_HEADS)][:, :, first : first + HEAD]

        def prepare(i, h):
            if i == 0:
                decay_diagonal[h] = keep.tile([P, P, PACK], F32, name="decay_diagonal%d" % h)
                nc.scalar.activation(
                    out=decay_diagonal[h][:], in_=steps_diagonal[:], func=ACT.Exp, scale=math.log(gammas[h])
                )
            if i == 1:
                decay_below[h] = keep.tile([P, P, PACK], F32, name="decay_below%d" % h)
                nc.scalar.activation(out=decay_below[h][:], in_=steps_below[:], func=ACT.Exp, scale=math.log(gammas[h]))
            flipped = psum_flip.tile([P, 2 * PACK, P], BF16)
            for t in range(PACK):
                nc.tensor.transpose(flipped[:, t, :], loaded(k_raw, i, h)[:, t, :], identity[:])
            for t in range(PACK):
                nc.tensor.transpose(flipped[:, PACK + t, :], loaded(q_raw, i, h)[:, t, :], identity[:])
            nc.scalar.copy(out=keys_t[i][:, h], in_=flipped[:, 0:PACK, :])
            q_t = work.tile([P, PACK, P], BF16, bufs=AHEAD + 2)
            nc.scalar.copy(out=q_t[:], in_=flipped[:, PACK : 2 * PACK, :])
            queries_t[(i, h)] = q_t

        def regroup_values(i, h):
            v_side = work.tile([P, HEAD, PACK], BF16, bufs=LAG + 2, align_bytes=64)
            nc.scalar.copy(out=v_side[:], in_=loaded(v_raw, i, h).rearrange("p t d -> p d t"))
            v_grouped[(i, h)] = v_side

        def decay_of(i, h, r, j):
            if j == i:
                return r + 1, 1.0, decay_diagonal[h][:, :, PACK - 1 - r : PACK]
            return PACK, gammas[h] ** (SPAN * (i - j - 1) + P * r), decay_below[h][:]

        def makes_detour(i, e, r, j):
            if j == i:
                return r < SHORT_DETOURS
            return e == 0

        def score(s):
            i, h, cells = rounds[s]
            banks[s] = []
            for e, (r, j) in enumerate(cells):
                strips, factor, table = decay_of(i, h, r, j)
                cell = psum_cell.tile([P, PACK, P], F32)
                for t in range(strips):
                    nc.tensor.matmul(
                        out=cell[:, t, :],
                        lhsT=keys_t[j][:, h, t, :],
                        rhs=queries_t[(i, h)][:, r, :],
                        start=True,
                        stop=True,
                    )
                banks[s].append(cell)
                if makes_detour(i, e, r, j):
                    taken_out = work.tile([P, P, strips], F32, bufs=4)
                    nc.scalar.mul(out=taken_out[:], in_=cell[:, 0:strips, :].rearrange("p t x -> p x t"), mul=factor)
                    scaled[(s, e)] = taken_out

        def apply_decay(s):
            i, h, cells = rounds[s]
            if cells[0][1] == i:
                side = diagonal_side[jobs.index((i, h)) % (LAG + 1)]
            else:
                side = work.tile([P, CELLS, P, PACK], BF16, bufs=LAG + 1, align_bytes=64)
            for e, (r, j) in enumerate(cells):
                strips, factor, table = decay_of(i, h, r, j)
                if makes_detour(i, e, r, j):
                    nc.gpsimd.tensor_tensor(out=side[:, e, :, 0:strips], in0=scaled[(s, e)][:], in1=table, op=ALU.mult)
                else:
                    nc.vector.scalar_tensor_tensor(
                        out=side[:, e, :, 0:strips],
                        in0=banks[s][e][:, 0:strips, :].rearrange("p t x -> p x t"),
                        scalar=factor,
                        in1=table,
                        op0=ALU.mult,
                        op1=ALU.mult,
                    )
            grouped[s] = side

        def quantise(s):
            i, h, cells = rounds[s]
            if cells[0][1] == i:
                nc.vector.quantize_mx(
                    out=v_codes[i][:, h, :].bitcast(FP8X4),
                    scales=v_scales[i][:, h, :],
                    in_=v_grouped[(i, h)][:].rearrange("p d t -> p (d t)"),
                )
                words = work.tile([P, CELLS, P], U32, name="diagonal_words", bufs=2, align_bytes=64)
                plane = work.tile([P, CELLS, P], U8, name="diagonal_plane", bufs=2, align_bytes=64)
                opening[(i, h)] = s
            else:
                words = work.tile([P, CELLS, P], U32, align_bytes=64)
                plane = work.tile([P, CELLS, P], U8, align_bytes=64)
            nc.vector.quantize_mx(
                out=words[:].rearrange("p e x -> p (e x)").bitcast(FP8X4),
                scales=plane[:].rearrange("p e x -> p (e x)"),
                in_=grouped[s][:].rearrange("p e x t -> p (e x t)"),
            )
            codes[s], scales[s] = words, plane

        def mx_pass(i, h, r, j, s, e, start, stop):
            nc.tensor.matmul_mx(
                out=products[(i, h)][:, r, :],
                lhsT=codes[s][:, e, :].bitcast(FP8X4),
                lhsT_scale=scales[s][:, e, :],
                rhs=v_codes[j][:, h, :].bitcast(FP8X4),
                rhs_scale=v_scales[j][:, h, :],
                start=start,
                stop=stop,
            )

        def multiply(s):
            i, h, cells = rounds[s]
            if cells[0] == (0, i):
                product = psum_out.tile([P, PACK, HEAD], F32)
                products[(i, h)] = product
            for e, (r, j) in enumerate(cells):
                if i == 0:
                    mx_pass(i, h, r, j, s, e, True, True)
                elif j < i:
                    if j == 0:
                        mx_pass(i, h, r, i, opening[(i, h)], r, True, False)
                    mx_pass(i, h, r, j, s, e, False, j == i - 1)
            if cells[-1] == (PACK - 1, max(i - 1, 0)):
                result = work.tile([P, PACK, HEAD], F32)
                nc.scalar.copy(out=result[:], in_=products[(i, h)][:])
                nc.sync.dma_start(
                    out=out_rows[i * SPAN : (i + 1) * SPAN, h * HEAD : (h + 1) * HEAD].rearrange(
                        "(r p) d -> p r d", p=P
                    ),
                    in_=result[:],
                )

        load_span(0)
        load_span(1)
        for i, h in jobs[0:AHEAD]:
            prepare(i, h)

        for s in range(len(rounds) + LAG + 1):
            if s < len(rounds):
                score(s)
                i, h, cells = rounds[s]
                if cells[0] == (0, i):
                    if h == 0 and 1 <= i < N_SPANS - 1:
                        load_span(i + 1)
                    regroup_values(i, h)
                    for later in jobs[jobs.index((i, h)) + AHEAD : jobs.index((i, h)) + AHEAD + 1]:
                        prepare(later[0], later[1])
            if 0 <= s - LAG - 1:
                multiply(s - LAG - 1)
            if s < len(rounds):
                apply_decay(s)
            if 0 <= s - LAG < len(rounds):
                quantise(s - LAG)
